import numpy as np
import ml_dtypes


def mxq(x, axis, fmt="e4m3"):
    dtype, down = {"e4m3": (ml_dtypes.float8_e4m3fn, 7), "e5m2": (ml_dtypes.float8_e5m2, 14)}[fmt]
    v = np.moveaxis(np.asarray(x, np.float32).astype(ml_dtypes.bfloat16).astype(np.float64), axis, -1)
    blocks = v.reshape(v.shape[:-1] + (-1, 32))
    amax = np.abs(blocks).max(-1, keepdims=True)
    byte = np.maximum(np.where(amax > 0, np.frexp(amax)[1] - 1 + 127, 0) - down, 1)
    scale = np.exp2(byte - 127.0)
    codes = (blocks / scale).astype(np.float32).astype(dtype).astype(np.float64)
    return np.moveaxis((codes * scale).reshape(v.shape), -1, axis)


WIDE = False


def mx_kscale(k):
    if not WIDE:
        return np.ones(k)
    levels = np.array([10, -10, 5, -5, 0])
    a = np.random.permutation(np.resize(levels, k // 512 * 4)).reshape(k // 512, 4)
    idx = np.arange(k)
    return np.exp2(a[idx // 512, idx % 128 // 32])


BF16 = ml_dtypes.bfloat16


def bf(x):
    return np.asarray(x, np.float32).astype(BF16)


def f64(x):
    return np.asarray(x).astype(np.float64)


B, NH, NW, C, K, P = 2, 4, 4, 512, 128, 4
T = P * P
HAD = np.array([[1.0, 1.0, 1.0, 1.0],
                [1.0, -1.0, 1.0, -1.0],
                [1.0, 1.0, -1.0, -1.0],
                [1.0, -1.0, -1.0, 1.0]])


def setup_inputs():
    s = mx_kscale(C)
    return {"trans": bf(np.random.standard_normal((T, B, NH, NW, C)) * s),
            "weight": bf(np.random.standard_normal((T, C, K)) * 0.5 * P / np.sqrt(C) / s[:, None]),
            "bias": bf(np.random.standard_normal((1, 1, 1, K)) * 0.2)}


def reference(trans, weight, bias):
    x = f64(trans).reshape(T, B * NH * NW, C)
    y = mxq(x, 2, "e4m3") @ mxq(f64(weight), 1, "e4m3")
    y = y.reshape(P, P, B, NH, NW, K)
    r = np.stack([sum(HAD[p, u] * y[u] for u in range(P)) for p in range(P)])
    z = np.stack([sum(HAD[q, v] * r[:, v] for v in range(P)) for q in range(P)], axis=1) / T
    z = z.transpose(2, 3, 0, 4, 1, 5)
    return z.reshape(B, P * NH, P * NW, K) + f64(bias)

@@ -1,0 +1,139 @@
+from contextlib import ExitStack
+
+import concourse.mybir as mybir
+from concourse.masks import make_identity
+
+F32 = mybir.dt.float32
+BF16 = mybir.dt.bfloat16
+U32 = mybir.dt.uint32
+U8 = mybir.dt.uint8
+FP8X4 = mybir.dt.float8_e4m3fn_x4
+ALU = mybir.AluOpType
+
+P = 128
+PACK = 4
+SIDE = 4
+ROWS = 32
+ROW_GROUPS = 8
+C = 512
+K = 128
+BANK = 512
+HAD = ((1, 1, 1, 1), (1, -1, 1, -1), (1, 1, -1, -1), (1, -1, -1, 1))
+
+K_GROUPS = K // 4
+SCALAR_GROUPS = 24
+
+FLOPS = 2 * SIDE * SIDE * ROWS * C * K
+
+
+def tile_iwht3layer_pa_s_kernel(tc, trans, weight, bias, out):
+    nc = tc.nc
+    with ExitStack() as ctx:
+        keep = ctx.enter_context(tc.tile_pool(name="keep", bufs=1))
+        psum = ctx.enter_context(tc.psum_pool(name="psum", bufs=1))
+
+        x_rows = keep.tile([P, SIDE, C], BF16)
+        nc.sync.dma_start(out=x_rows[:], in_=trans.rearrange("(u v) b i j c -> (v b i j) u c", v=SIDE))
+
+        w_view = weight.rearrange("(u v) (c4 s) k -> v c4 u (s k)", v=SIDE, s=PACK)
+        w_raw = {}
+        for v in range(SIDE):
+            for uh in range(2):
+                w_raw[v, uh] = keep.tile([P, 2, PACK * K], BF16, name="w_raw_%d_%d" % (v, uh))
+                nc.sync.dma_start(out=w_raw[v, uh][:], in_=w_view[v, :, 2 * uh : 2 * uh + 2, :])
+
+        identity = keep.tile([P, P], F32)
+        make_identity(nc, identity[:])
+        ones = keep.tile([P, P], BF16)
+        nc.vector.memset(ones[:], 1.0)
+        bias_rows = keep.tile([P, K], BF16)
+        nc.vector.memset(bias_rows[:], 0.0)
+        nc.scalar.dma_start(out=bias_rows[0:1, :], in_=bias.rearrange("a b c k -> (a b c) k"))
+        bias_bank = psum.tile([P, BANK], F32)
+        nc.tensor.matmul(out=bias_bank[:, :K], lhsT=ones[:], rhs=bias_rows[:], start=True, stop=True)
+        bias_all = keep.tile([P, K], F32)
+        nc.scalar.copy(out=bias_all[:], in_=bias_bank[:, :K])
+
+        x_words = x_rows[:].bitcast(F32).rearrange("m u (c4 h) -> m u h c4", h=2)
+        signed = keep.tile([P, SIDE, SIDE * ROW_GROUPS, SIDE, SIDE * PACK], BF16, align_bytes=64)
+        signed_words = signed[:].bitcast(F32).rearrange("c u g p (j h) -> c u g p j h", h=2)
+        for uh in range(2):
+            x_bank = psum.tile([P, 2, 2, P], F32, name="x_bank_%d" % uh)
+            for ul in range(2):
+                for h in range(2):
+                    nc.tensor.transpose(x_bank[:, h, ul, :], x_words[:, 2 * uh + ul, h, :], identity[:])
+            copy_out = nc.vector.tensor_copy if uh == 0 else nc.scalar.copy
+            copy_out(
+                out=signed_words[:, 2 * uh : 2 * uh + 2, :, 0, :, :],
+                in_=x_bank[:].rearrange("c h ul (g j) -> c ul g j h", j=SIDE),
+            )
+
+        x_codes = keep.tile([P, SIDE, SIDE * P], U32, align_bytes=64)
+        x_scales = keep.tile([P, SIDE, SIDE * P], U8, align_bytes=64)
+        for u in range(SIDE):
+            for p in range(1, SIDE):
+                nc.vector.tensor_scalar_mul(
+                    out=signed[:, u, :, p, :], in0=signed[:, u, :, 0, :], scalar1=float(HAD[p][u])
+                )
+        for u in range(SIDE):
+            nc.vector.quantize_mx(
+                out=x_codes[:, u, :].bitcast(FP8X4),
+                scales=x_scales[:, u, :],
+                in_=signed[:, u].rearrange("c g p e -> c (g p e)"),
+            )
+
+        w_codes = keep.tile([P, SIDE, SIDE, K], U32, align_bytes=64)
+        w_scales = keep.tile([P, SIDE, SIDE, K], U8, align_bytes=64)
+        half = [psum.tile([P, BANK], F32, name="half_%d" % v) for v in range(SIDE)]
+        first = keep.tile([P, K], F32)
+        pair01 = keep.tile([P, 2, K], F32)
+        third = keep.tile([P, K], F32)
+        pair23 = keep.tile([P, 2, K], F32)
+        result = keep.tile([P, SIDE, K], F32)
+
+        for v in range(SIDE):
+            for uh in range(2):
+                grouped = keep.tile([P, 2, K, PACK], BF16, name="grouped_%d_%d" % (v, uh), align_bytes=64)
+                for ul in range(2):
+                    src = w_raw[v, uh][:, ul, :].rearrange("c (s g i) -> c g s i", s=PACK, i=4)
+                    dst = grouped[:, ul].rearrange("c (g i) s -> c g s i", i=4)
+                    nc.scalar.copy(out=dst[:, :SCALAR_GROUPS], in_=src[:, :SCALAR_GROUPS])
+                    nc.vector.tensor_copy(out=dst[:, SCALAR_GROUPS:], in_=src[:, SCALAR_GROUPS:])
+                nc.vector.quantize_mx(
+                    out=w_codes[:, v, 2 * uh : 2 * uh + 2, :].rearrange("c u k -> c (u k)").bitcast(FP8X4),
+                    scales=w_scales[:, v, 2 * uh : 2 * uh + 2, :].rearrange("c u k -> c (u k)"),
+                    in_=grouped[:].rearrange("c u k s -> c (u k s)"),
+                )
+                for u in (2 * uh, 2 * uh + 1):
+                    nc.tensor.matmul_mx(
+                        out=half[v][:, :K],
+                        lhsT=x_codes[:, u, v * P : (v + 1) * P].bitcast(FP8X4),
+                        lhsT_scale=x_scales[:, u, v * P : (v + 1) * P],
+                        rhs=w_codes[:, v, u, :].bitcast(FP8X4),
+                        rhs_scale=w_scales[:, v, u, :],
+                        start=(u == 0),
+                        stop=(u == SIDE - 1),
+                    )
+            if v == 0:
+                nc.vector.scalar_tensor_tensor(
+                    out=first[:], in0=half[0][:, :K], scalar=1.0 / 16.0, in1=bias_all[:], op0=ALU.mult, op1=ALU.add
+                )
+            if v == 1:
+                for e, factor in enumerate((1.0 / 16.0, -1.0 / 16.0)):
+                    nc.vector.scalar_tensor_tensor(
+                        out=pair01[:, e, :], in0=half[1][:, :K], scalar=factor, in1=first[:], op0=ALU.mult, op1=ALU.add
+                    )
+            if v == 2:
+                nc.scalar.copy(out=third[:], in_=half[2][:, :K])
+            if v == 3:
+                nc.vector.tensor_tensor(out=pair23[:, 0, :], in0=third[:], in1=half[3][:, :K], op=ALU.add)
+                nc.vector.tensor_tensor(out=pair23[:, 1, :], in0=third[:], in1=half[3][:, :K], op=ALU.subtract)
+
+        for e, factor in enumerate((1.0 / 16.0, -1.0 / 16.0)):
+            nc.vector.scalar_tensor_tensor(
+                out=result[:, 2 * e : 2 * e + 2, :], in0=pair23[:], scalar=factor, in1=pair01[:], op0=ALU.mult, op1=ALU.add
+            )
+        nc.sync.dma_start(
+            out=out.rearrange("b (i p) (j q) k -> (b i p j) (q k)", p=SIDE, q=SIDE),
+            in_=result[:].rearrange("m q k -> m (q k)"),
+        )

@@ -20,9 +20,6 @@ K = 128
 BANK = 512
 HAD = ((1, 1, 1, 1), (1, -1, 1, -1), (1, 1, -1, -1), (1, -1, -1, 1))
 
-K_GROUPS = K // 4
-SCALAR_GROUPS = 24
-
 FLOPS = 2 * SIDE * SIDE * ROWS * C * K
 
 
@@ -31,16 +28,19 @@ def tile_iwht3layer_pa_s_kernel(tc, trans, weight, bias, out):
     with ExitStack() as ctx:
         keep = ctx.enter_context(tc.tile_pool(name="keep", bufs=1))
         psum = ctx.enter_context(tc.psum_pool(name="psum", bufs=1))
+        ctx.enter_context(tc.manual_schedule())
+
+        pieces = [(v, uh) for v in range(SIDE) for uh in range(2)]
 
         x_rows = keep.tile([P, SIDE, C], BF16)
-        nc.sync.dma_start(out=x_rows[:], in_=trans.rearrange("(u v) b i j c -> (v b i j) u c", v=SIDE))
-
+        x_view = trans.rearrange("(u v) b i j c -> (v b i j) u c", v=SIDE)
+        for u in range(SIDE):
+            nc.sync.dma_start(out=x_rows[:, u, :], in_=x_view[:, u, :])
         w_view = weight.rearrange("(u v) (c4 s) k -> v c4 u (s k)", v=SIDE, s=PACK)
         w_raw = {}
-        for v in range(SIDE):
-            for uh in range(2):
-                w_raw[v, uh] = keep.tile([P, 2, PACK * K], BF16, name="w_raw_%d_%d" % (v, uh))
-                nc.sync.dma_start(out=w_raw[v, uh][:], in_=w_view[v, :, 2 * uh : 2 * uh + 2, :])
+        for v, uh in pieces:
+            w_raw[v, uh] = keep.tile([P, 2, PACK * K], BF16, name="w_raw_%d_%d" % (v, uh))
+            nc.sync.dma_start(out=w_raw[v, uh][:], in_=w_view[v, :, 2 * uh : 2 * uh + 2, :])
 
         identity = keep.tile([P, P], F32)
         make_identity(nc, identity[:])
@@ -49,7 +49,7 @@ def tile_iwht3layer_pa_s_kernel(tc, trans, weight, bias, out):
         bias_rows = keep.tile([P, K], BF16)
         nc.vector.memset(bias_rows[:], 0.0)
         nc.scalar.dma_start(out=bias_rows[0:1, :], in_=bias.rearrange("a b c k -> (a b c) k"))
-        bias_bank = psum.tile([P, BANK], F32)
+        bias_bank = psum.tile([P, BANK], F32, tag="x_bank_3")
         nc.tensor.matmul(out=bias_bank[:, :K], lhsT=ones[:], rhs=bias_rows[:], start=True, stop=True)
         bias_all = keep.tile([P, K], F32)
         nc.scalar.copy(out=bias_all[:], in_=bias_bank[:, :K])
@@ -57,30 +57,45 @@ def tile_iwht3layer_pa_s_kernel(tc, trans, weight, bias, out):
         x_words = x_rows[:].bitcast(F32).rearrange("m u (c4 h) -> m u h c4", h=2)
         signed = keep.tile([P, SIDE, SIDE * ROW_GROUPS, SIDE, SIDE * PACK], BF16, align_bytes=64)
         signed_words = signed[:].bitcast(F32).rearrange("c u g p (j h) -> c u g p j h", h=2)
-        for uh in range(2):
-            x_bank = psum.tile([P, 2, 2, P], F32, name="x_bank_%d" % uh)
-            for ul in range(2):
-                for h in range(2):
-                    nc.tensor.transpose(x_bank[:, h, ul, :], x_words[:, 2 * uh + ul, h, :], identity[:])
-            copy_out = nc.vector.tensor_copy if uh == 0 else nc.scalar.copy
-            copy_out(
-                out=signed_words[:, 2 * uh : 2 * uh + 2, :, 0, :, :],
-                in_=x_bank[:].rearrange("c h ul (g j) -> c ul g j h", j=SIDE),
-            )
-
         x_codes = keep.tile([P, SIDE, SIDE * P], U32, align_bytes=64)
         x_scales = keep.tile([P, SIDE, SIDE * P], U8, align_bytes=64)
-        for u in range(SIDE):
-            for p in range(1, SIDE):
-                nc.vector.tensor_scalar_mul(
-                    out=signed[:, u, :, p, :], in0=signed[:, u, :, 0, :], scalar1=float(HAD[p][u])
-                )
-        for u in range(SIDE):
+
+        def quantise_x(u):
             nc.vector.quantize_mx(
                 out=x_codes[:, u, :].bitcast(FP8X4),
                 scales=x_scales[:, u, :],
                 in_=signed[:, u].rearrange("c g p e -> c (g p e)"),
             )
+
+        for u in range(SIDE):
+            x_bank = psum.tile([P, BANK], F32, tag="x_bank_%d" % u)
+            for h in range(2):
+                nc.tensor.transpose(x_bank[:, h * P : (h + 1) * P], x_words[:, u, h, :], identity[:])
+            nc.scalar.copy(
+                out=signed_words[:, u, :, 0, :, :],
+                in_=x_bank[:, : 2 * P].rearrange("c (h g j) -> c g j h", h=2, j=SIDE),
+            )
+            for p in range(1, SIDE):
+                nc.vector.tensor_scalar_mul(
+                    out=signed[:, u, :, p, :], in0=signed[:, u, :, 0, :], scalar1=float(HAD[p][u])
+                )
+            if u >= 1:
+                quantise_x(u - 1)
+        quantise_x(SIDE - 1)
+
+        grouped = {}
+        for v, uh in pieces:
+            grouped[v, uh] = keep.tile([P, 2, K, PACK], BF16, name="grouped_%d_%d" % (v, uh), align_bytes=64)
+
+        def regroup(copy, v, u):
+            copy(
+                out=grouped[v, u // 2][:, u % 2].rearrange("c (g i) s -> c g s i", i=4),
+                in_=w_raw[v, u // 2][:, u % 2, :].rearrange("c (s g i) -> c g s i", s=PACK, i=4),
+            )
+
+        for v in range(SIDE):
+            for u in range(SIDE - 1):
+                regroup(nc.scalar.copy, v, u)
 
         w_codes = keep.tile([P, SIDE, SIDE, K], U32, align_bytes=64)
         w_scales = keep.tile([P, SIDE, SIDE, K], U8, align_bytes=64)
@@ -91,29 +106,7 @@ def tile_iwht3layer_pa_s_kernel(tc, trans, weight, bias, out):
         pair23 = keep.tile([P, 2, K], F32)
         result = keep.tile([P, SIDE, K], F32)
 
-        for v in range(SIDE):
-            for uh in range(2):
-                grouped = keep.tile([P, 2, K, PACK], BF16, name="grouped_%d_%d" % (v, uh), align_bytes=64)
-                for ul in range(2):
-                    src = w_raw[v, uh][:, ul, :].rearrange("c (s g i) -> c g s i", s=PACK, i=4)
-                    dst = grouped[:, ul].rearrange("c (g i) s -> c g s i", i=4)
-                    nc.scalar.copy(out=dst[:, :SCALAR_GROUPS], in_=src[:, :SCALAR_GROUPS])
-                    nc.vector.tensor_copy(out=dst[:, SCALAR_GROUPS:], in_=src[:, SCALAR_GROUPS:])
-                nc.vector.quantize_mx(
-                    out=w_codes[:, v, 2 * uh : 2 * uh + 2, :].rearrange("c u k -> c (u k)").bitcast(FP8X4),
-                    scales=w_scales[:, v, 2 * uh : 2 * uh + 2, :].rearrange("c u k -> c (u k)"),
-                    in_=grouped[:].rearrange("c u k s -> c (u k s)"),
-                )
-                for u in (2 * uh, 2 * uh + 1):
-                    nc.tensor.matmul_mx(
-                        out=half[v][:, :K],
-                        lhsT=x_codes[:, u, v * P : (v + 1) * P].bitcast(FP8X4),
-                        lhsT_scale=x_scales[:, u, v * P : (v + 1) * P],
-                        rhs=w_codes[:, v, u, :].bitcast(FP8X4),
-                        rhs_scale=w_scales[:, v, u, :],
-                        start=(u == 0),
-                        stop=(u == SIDE - 1),
-                    )
+        def combine(v):
             if v == 0:
                 nc.vector.scalar_tensor_tensor(
                     out=first[:], in0=half[0][:, :K], scalar=1.0 / 16.0, in1=bias_all[:], op0=ALU.mult, op1=ALU.add
@@ -128,6 +121,28 @@ def tile_iwht3layer_pa_s_kernel(tc, trans, weight, bias, out):
             if v == 3:
                 nc.vector.tensor_tensor(out=pair23[:, 0, :], in0=third[:], in1=half[3][:, :K], op=ALU.add)
                 nc.vector.tensor_tensor(out=pair23[:, 1, :], in0=third[:], in1=half[3][:, :K], op=ALU.subtract)
+
+        for v, uh in pieces:
+            if uh == 0:
+                regroup(nc.vector.tensor_copy, v, SIDE - 1)
+            nc.vector.quantize_mx(
+                out=w_codes[:, v, 2 * uh : 2 * uh + 2, :].rearrange("c u k -> c (u k)").bitcast(FP8X4),
+                scales=w_scales[:, v, 2 * uh : 2 * uh + 2, :].rearrange("c u k -> c (u k)"),
+                in_=grouped[v, uh][:].rearrange("c u k s -> c (u k s)"),
+            )
+            for u in (2 * uh, 2 * uh + 1):
+                nc.tensor.matmul_mx(
+                    out=half[v][:, :K],
+                    lhsT=x_codes[:, u, v * P : (v + 1) * P].bitcast(FP8X4),
+                    lhsT_scale=x_scales[:, u, v * P : (v + 1) * P],
+                    rhs=w_codes[:, v, u, :].bitcast(FP8X4),
+                    rhs_scale=w_scales[:, v, u, :],
+                    start=(u == 0),
+                    stop=(u == SIDE - 1),
+                )
+            if uh == 0 and v >= 1:
+                combine(v - 1)
+        combine(SIDE - 1)
 
         for e, factor in enumerate((1.0 / 16.0, -1.0 / 16.0)):
             nc.vector.scalar_tensor_tensor(

@@ -100,27 +100,28 @@ def tile_iwht3layer_pa_s_kernel(tc, trans, weight, bias, out):
         w_codes = keep.tile([P, SIDE, SIDE, K], U32, align_bytes=64)
         w_scales = keep.tile([P, SIDE, SIDE, K], U8, align_bytes=64)
         half = [psum.tile([P, BANK], F32, name="half_%d" % v) for v in range(SIDE)]
-        first = keep.tile([P, K], F32)
-        pair01 = keep.tile([P, 2, K], F32)
-        third = keep.tile([P, K], F32)
-        pair23 = keep.tile([P, 2, K], F32)
-        result = keep.tile([P, SIDE, K], F32)
+        total = [keep.tile([P, min(2**v, SIDE), K], F32, name="total_%d" % v) for v in range(SIDE)]
 
         def combine(v):
             if v == 0:
                 nc.vector.scalar_tensor_tensor(
-                    out=first[:], in0=half[0][:, :K], scalar=1.0 / 16.0, in1=bias_all[:], op0=ALU.mult, op1=ALU.add
+                    out=total[0][:, 0, :], in0=half[0][:, :K], scalar=1.0 / 16.0, in1=bias_all[:], op0=ALU.mult, op1=ALU.add
                 )
             if v == 1:
-                for e, factor in enumerate((1.0 / 16.0, -1.0 / 16.0)):
+                for q in range(2):
                     nc.vector.scalar_tensor_tensor(
-                        out=pair01[:, e, :], in0=half[1][:, :K], scalar=factor, in1=first[:], op0=ALU.mult, op1=ALU.add
+                        out=total[1][:, q, :], in0=half[1][:, :K], scalar=HAD[q][1] / 16.0, in1=total[0][:, 0, :],
+                        op0=ALU.mult, op1=ALU.add,
                     )
-            if v == 2:
-                nc.scalar.copy(out=third[:], in_=half[2][:, :K])
-            if v == 3:
-                nc.vector.tensor_tensor(out=pair23[:, 0, :], in0=third[:], in1=half[3][:, :K], op=ALU.add)
-                nc.vector.tensor_tensor(out=pair23[:, 1, :], in0=third[:], in1=half[3][:, :K], op=ALU.subtract)
+            if v >= 2:
+                twice = half[v][:, :K].unsqueeze(1).to_broadcast([P, 2, K])
+                for sign in (1, -1):
+                    first, second = [q for q in range(SIDE) if HAD[q][v] == sign]
+                    pair = slice(first, second + 1, second - first)
+                    before = total[1][:] if v == 2 else total[2][:, pair, :]
+                    nc.vector.scalar_tensor_tensor(
+                        out=total[v][:, pair, :], in0=twice, scalar=sign / 16.0, in1=before, op0=ALU.mult, op1=ALU.add
+                    )
 
         for v, uh in pieces:
             if uh == 0:
@@ -140,15 +141,11 @@ def tile_iwht3layer_pa_s_kernel(tc, trans, weight, bias, out):
                     start=(u == 0),
                     stop=(u == SIDE - 1),
                 )
-            if uh == 0 and v >= 1:
+            if uh == 1 and v >= 1:
                 combine(v - 1)
         combine(SIDE - 1)
 
-        for e, factor in enumerate((1.0 / 16.0, -1.0 / 16.0)):
-            nc.vector.scalar_tensor_tensor(
-                out=result[:, 2 * e : 2 * e + 2, :], in0=pair23[:], scalar=factor, in1=pair01[:], op0=ALU.mult, op1=ALU.add
-            )
         nc.sync.dma_start(
             out=out.rearrange("b (i p) (j q) k -> (b i p j) (q k)", p=SIDE, q=SIDE),
-            in_=result[:].rearrange("m q k -> m (q k)"),
+            in_=total[SIDE - 1][:].rearrange("m q k -> m (q k)"),
         )

@@ -94,7 +94,7 @@ def tile_iwht3layer_pa_s_kernel(tc, trans, weight, bias, out):
             )
 
         for v in range(SIDE):
-            for u in range(SIDE - 1):
+            for u in range(SIDE if v == 0 else SIDE - 1):
                 regroup(nc.scalar.copy, v, u)
 
         w_codes = keep.tile([P, SIDE, SIDE, K], U32, align_bytes=64)
@@ -124,7 +124,7 @@ def tile_iwht3layer_pa_s_kernel(tc, trans, weight, bias, out):
                     )
 
         for v, uh in pieces:
-            if uh == 0:
+            if uh == 0 and v >= 1:
                 regroup(nc.vector.tensor_copy, v, SIDE - 1)
             nc.vector.quantize_mx(
                 out=w_codes[:, v, 2 * uh : 2 * uh + 2, :].rearrange("c u k -> c (u k)").bitcast(FP8X4),

@@ -49,10 +49,6 @@ def tile_iwht3layer_pa_s_kernel(tc, trans, weight, bias, out):
         bias_rows = keep.tile([P, K], BF16)
         nc.vector.memset(bias_rows[:], 0.0)
         nc.scalar.dma_start(out=bias_rows[0:1, :], in_=bias.rearrange("a b c k -> (a b c) k"))
-        bias_bank = psum.tile([P, BANK], F32, tag="x_bank_3")
-        nc.tensor.matmul(out=bias_bank[:, :K], lhsT=ones[:], rhs=bias_rows[:], start=True, stop=True)
-        bias_all = keep.tile([P, K], F32)
-        nc.scalar.copy(out=bias_all[:], in_=bias_bank[:, :K])
 
         x_words = x_rows[:].bitcast(F32).rearrange("m u (c4 h) -> m u h c4", h=2)
         signed = keep.tile([P, SIDE, SIDE * ROW_GROUPS, SIDE, SIDE * PACK], BF16, align_bytes=64)
@@ -83,6 +79,11 @@ def tile_iwht3layer_pa_s_kernel(tc, trans, weight, bias, out):
                 quantise_x(u - 1)
         quantise_x(SIDE - 1)
 
+        bias_bank = psum.tile([P, BANK], F32, tag="half_3")
+        nc.tensor.matmul(out=bias_bank[:, :K], lhsT=ones[:], rhs=bias_rows[:], start=True, stop=True)
+        bias_all = keep.tile([P, K], F32)
+        nc.scalar.copy(out=bias_all[:], in_=bias_bank[:, :K])
+
         grouped = {}
         for v, uh in pieces:
             grouped[v, uh] = keep.tile([P, 2, K, PACK], BF16, name="grouped_%d_%d" % (v, uh), align_bytes=64)
@@ -101,6 +102,8 @@ def tile_iwht3layer_pa_s_kernel(tc, trans, weight, bias, out):
         w_scales = keep.tile([P, SIDE, SIDE, K], U8, align_bytes=64)
         half = [psum.tile([P, BANK], F32, name="half_%d" % v) for v in range(SIDE)]
         total = [keep.tile([P, min(2**v, SIDE), K], F32, name="total_%d" % v) for v in range(SIDE)]
+
+        out_view = out.rearrange("b (i p) (j q) k -> (b i p j) q k", p=SIDE, q=SIDE)
 
         def combine(v):
             if v == 0:
@@ -122,6 +125,8 @@ def tile_iwht3layer_pa_s_kernel(tc, trans, weight, bias, out):
                     nc.vector.scalar_tensor_tensor(
                         out=total[v][:, pair, :], in0=twice, scalar=sign / 16.0, in1=before, op0=ALU.mult, op1=ALU.add
                     )
+                    if v == SIDE - 1:
+                        nc.sync.dma_start(out=out_view[:, pair, :], in_=total[v][:, pair, :])
 
         for v, uh in pieces:
             if uh == 0 and v >= 1:
@@ -144,8 +149,3 @@ def tile_iwht3layer_pa_s_kernel(tc, trans, weight, bias, out):
             if uh == 1 and v >= 1:
                 combine(v - 1)
         combine(SIDE - 1)
-
-        nc.sync.dma_start(
-            out=out.rearrange("b (i p) (j q) k -> (b i p j) (q k)", p=SIDE, q=SIDE),
-            in_=total[SIDE - 1][:].rearrange("m q k -> m (q k)"),
-        )

@@ -6,6 +6,7 @@ from concourse.masks import make_identity
 F32 = mybir.dt.float32
 BF16 = mybir.dt.bfloat16
 U32 = mybir.dt.uint32
+I32 = mybir.dt.int32
 U8 = mybir.dt.uint8
 FP8X4 = mybir.dt.float8_e4m3fn_x4
 ALU = mybir.AluOpType
@@ -51,61 +52,123 @@ def tile_iwht3layer_pa_s_kernel(tc, trans, weight, bias, out):
         nc.scalar.dma_start(out=bias_rows[0:1, :], in_=bias.rearrange("a b c k -> (a b c) k"))
 
         x_words = x_rows[:].bitcast(F32).rearrange("m u (c4 h) -> m u h c4", h=2)
-        signed = keep.tile([P, SIDE, SIDE * ROW_GROUPS, SIDE, SIDE * PACK], BF16, align_bytes=64)
-        signed_words = signed[:].bitcast(F32).rearrange("c u g p (j h) -> c u g p j h", h=2)
-        x_codes = keep.tile([P, SIDE, SIDE * P], U32, align_bytes=64)
+        GROUPS = SIDE * ROW_GROUPS
+        plain = keep.tile([P, P * PACK], BF16, align_bytes=64)
+        plain_codes = keep.tile([P, P], I32, align_bytes=64)
+        plain_scales = keep.tile([P, P], U8, align_bytes=64)
+        both = keep.tile([P, SIDE - 1, GROUPS, 2, SIDE * PACK], BF16, align_bytes=64)
+        both_codes = keep.tile([P, SIDE - 1, GROUPS, 2, SIDE], I32, align_bytes=64)
+        both_scales = keep.tile([P, SIDE - 1, GROUPS * 2 * SIDE], U8, align_bytes=64)
+        nc.vector.memset(plain_scales[:].bitcast(I32), 0)
+        nc.vector.memset(both_scales[:].bitcast(I32), 0)
+        x_codes = keep.tile([P, SIDE, SIDE * P], I32, align_bytes=64)
         x_scales = keep.tile([P, SIDE, SIDE * P], U8, align_bytes=64)
 
+        def negate(u):
+            nc.vector.tensor_scalar_mul(out=both[:, u - 1, :, 1, :], in0=both[:, u - 1, :, 0, :], scalar1=-1.0)
+
         def quantise_x(u):
-            nc.vector.quantize_mx(
-                out=x_codes[:, u, :].bitcast(FP8X4),
-                scales=x_scales[:, u, :],
-                in_=signed[:, u].rearrange("c g p e -> c (g p e)"),
+            if u == 0:
+                nc.vector.quantize_mx(out=plain_codes[:].bitcast(FP8X4), scales=plain_scales[:], in_=plain[:])
+            else:
+                nc.vector.quantize_mx(
+                    out=both_codes[:, u - 1].rearrange("c g n j -> c (g n j)").bitcast(FP8X4),
+                    scales=both_scales[:, u - 1, :],
+                    in_=both[:, u - 1].rearrange("c g n e -> c (g n e)"),
+                )
+
+        def spread(u):
+            codes = x_codes[:, u, :]
+            if u == 0:
+                nc.vector.tensor_copy(
+                    out=codes.rearrange("c (g p j) -> c g p j", p=SIDE, j=SIDE),
+                    in_=plain_codes[:].rearrange("c (g j) -> c g j", j=SIDE).unsqueeze(2).to_broadcast([P, GROUPS, SIDE, SIDE]),
+                )
+            if u == 1:
+                nc.vector.tensor_copy(
+                    out=codes.rearrange("c (g a e) -> c g a e", a=2, e=2 * SIDE),
+                    in_=both_codes[:, 0].rearrange("c g n j -> c g (n j)").unsqueeze(2).to_broadcast([P, GROUPS, 2, 2 * SIDE]),
+                )
+            if u == 2:
+                nc.vector.tensor_copy(
+                    out=codes.rearrange("c (m a j) -> c m a j", a=2, j=SIDE),
+                    in_=both_codes[:, 1].rearrange("c g n j -> c (g n) j").unsqueeze(2).to_broadcast([P, 2 * GROUPS, 2, SIDE]),
+                )
+            if u == 3:
+                for n, where in enumerate((slice(0, SIDE, SIDE - 1), slice(1, SIDE - 1))):
+                    nc.vector.tensor_copy(
+                        out=codes.rearrange("c (g p j) -> c g p j", p=SIDE, j=SIDE)[:, :, where, :],
+                        in_=both_codes[:, 2, :, n, :].unsqueeze(2).to_broadcast([P, GROUPS, 2, SIDE]),
+                    )
+
+        def spread_scales():
+            nc.vector.tensor_copy(
+                out=x_scales[:, 0, :].bitcast(I32).rearrange("c (g p) -> c g p", p=SIDE),
+                in_=plain_scales[:].bitcast(I32).unsqueeze(2).to_broadcast([P, GROUPS, SIDE]),
+            )
+            nc.vector.tensor_copy(
+                out=x_scales[:, 1:, :].bitcast(I32).rearrange("c u (g p) -> c u g p", p=SIDE),
+                in_=both_scales[:].bitcast(I32).rearrange("c u (g n) -> c u g n", n=2)[:, :, :, 0:1].to_broadcast([P, SIDE - 1, GROUPS, SIDE]),
             )
 
         for u in range(SIDE):
             x_bank = psum.tile([P, BANK], F32, tag="x_bank_%d" % u)
             for h in range(2):
                 nc.tensor.transpose(x_bank[:, h * P : (h + 1) * P], x_words[:, u, h, :], identity[:])
-            nc.scalar.copy(
-                out=signed_words[:, u, :, 0, :, :],
-                in_=x_bank[:, : 2 * P].rearrange("c (h g j) -> c g j h", h=2, j=SIDE),
-            )
-            for p in range(1, SIDE):
-                nc.vector.tensor_scalar_mul(
-                    out=signed[:, u, :, p, :], in0=signed[:, u, :, 0, :], scalar1=float(HAD[p][u])
+            if u == 0:
+                nc.scalar.copy(
+                    out=plain[:].bitcast(F32).rearrange("c (m h) -> c m h", h=2),
+                    in_=x_bank[:, : 2 * P].rearrange("c (h m) -> c m h", h=2),
                 )
-            if u >= 1:
-                quantise_x(u - 1)
-        quantise_x(SIDE - 1)
+            else:
+                nc.scalar.copy(
+                    out=both[:, u - 1, :, 0, :].bitcast(F32).rearrange("c g (j h) -> c g j h", h=2),
+                    in_=x_bank[:, : 2 * P].rearrange("c (h g j) -> c g j h", h=2, j=SIDE),
+                )
+        for u in range(SIDE):
+            quantise_x(u)
+            if u + 1 < SIDE:
+                negate(u + 1)
+                spread(u)
 
         bias_bank = psum.tile([P, BANK], F32, tag="half_3")
         nc.tensor.matmul(out=bias_bank[:, :K], lhsT=ones[:], rhs=bias_rows[:], start=True, stop=True)
         bias_all = keep.tile([P, K], F32)
         nc.scalar.copy(out=bias_all[:], in_=bias_bank[:, :K])
 
+        groups = []
+        for v in range(SIDE - 1):
+            groups.extend([[(v, 0), (v, 1)], [(v, 2), (v, 3)]])
+        groups.extend([[(SIDE - 1, 0), (SIDE - 1, 3)], [(SIDE - 1, 1)], [(SIDE - 1, 2)]])
+        group_tiles = []
         grouped = {}
-        for v, uh in pieces:
-            grouped[v, uh] = keep.tile([P, 2, K, PACK], BF16, name="grouped_%d_%d" % (v, uh), align_bytes=64)
+        column = {}
+        filled = 0
+        for n, members in enumerate(groups):
+            group_tiles.append(keep.tile([P, len(members), K, PACK], BF16, name="grouped_%d" % n, align_bytes=64))
+            for slot, vu in enumerate(members):
+                grouped[vu] = group_tiles[n][:, slot]
+                column[vu] = filled + slot * K
+            filled += len(members) * K
 
         def regroup(copy, v, u):
             copy(
-                out=grouped[v, u // 2][:, u % 2].rearrange("c (g i) s -> c g s i", i=4),
+                out=grouped[v, u].rearrange("c (g i) s -> c g s i", i=4),
                 in_=w_raw[v, u // 2][:, u % 2, :].rearrange("c (s g i) -> c g s i", s=PACK, i=4),
             )
 
         for v in range(SIDE):
-            for u in range(SIDE if v == 0 else SIDE - 1):
+            for u in range(SIDE - 1):
                 regroup(nc.scalar.copy, v, u)
 
-        w_codes = keep.tile([P, SIDE, SIDE, K], U32, align_bytes=64)
-        w_scales = keep.tile([P, SIDE, SIDE, K], U8, align_bytes=64)
+        w_codes = keep.tile([P, SIDE * SIDE * K], U32, align_bytes=64)
+        w_scales = keep.tile([P, SIDE * SIDE * K], U8, align_bytes=64)
         half = [psum.tile([P, BANK], F32, name="half_%d" % v) for v in range(SIDE)]
         total = [keep.tile([P, min(2**v, SIDE), K], F32, name="total_%d" % v) for v in range(SIDE)]
 
         out_view = out.rearrange("b (i p) (j q) k -> (b i p j) q k", p=SIDE, q=SIDE)
 
-        def combine(v):
+        def combine(v, signs=(1, -1)):
             if v == 0:
                 nc.vector.scalar_tensor_tensor(
                     out=total[0][:, 0, :], in0=half[0][:, :K], scalar=1.0 / 16.0, in1=bias_all[:], op0=ALU.mult, op1=ALU.add
@@ -118,7 +181,7 @@ def tile_iwht3layer_pa_s_kernel(tc, trans, weight, bias, out):
                     )
             if v >= 2:
                 twice = half[v][:, :K].unsqueeze(1).to_broadcast([P, 2, K])
-                for sign in (1, -1):
+                for sign in signs:
                     first, second = [q for q in range(SIDE) if HAD[q][v] == sign]
                     pair = slice(first, second + 1, second - first)
                     before = total[1][:] if v == 2 else total[2][:, pair, :]
@@ -128,24 +191,32 @@ def tile_iwht3layer_pa_s_kernel(tc, trans, weight, bias, out):
                     if v == SIDE - 1:
                         nc.sync.dma_start(out=out_view[:, pair, :], in_=total[v][:, pair, :])
 
-        for v, uh in pieces:
-            if uh == 0 and v >= 1:
+        passes = [0] * SIDE
+        for n, members in enumerate(groups):
+            v = members[0][0]
+            if passes[v] == 0:
                 regroup(nc.vector.tensor_copy, v, SIDE - 1)
+                if v == 0:
+                    spread(SIDE - 1)
+                    spread_scales()
+            columns = slice(column[members[0]], column[members[0]] + len(members) * K)
             nc.vector.quantize_mx(
-                out=w_codes[:, v, 2 * uh : 2 * uh + 2, :].rearrange("c u k -> c (u k)").bitcast(FP8X4),
-                scales=w_scales[:, v, 2 * uh : 2 * uh + 2, :].rearrange("c u k -> c (u k)"),
-                in_=grouped[v, uh][:].rearrange("c u k s -> c (u k s)"),
+                out=w_codes[:, columns].bitcast(FP8X4),
+                scales=w_scales[:, columns],
+                in_=group_tiles[n][:].rearrange("c u k s -> c (u k s)"),
             )
-            for u in (2 * uh, 2 * uh + 1):
+            for vu in members:
+                u = vu[1]
                 nc.tensor.matmul_mx(
                     out=half[v][:, :K],
                     lhsT=x_codes[:, u, v * P : (v + 1) * P].bitcast(FP8X4),
                     lhsT_scale=x_scales[:, u, v * P : (v + 1) * P],
-                    rhs=w_codes[:, v, u, :].bitcast(FP8X4),
-                    rhs_scale=w_scales[:, v, u, :],
-                    start=(u == 0),
-                    stop=(u == SIDE - 1),
+                    rhs=w_codes[:, column[vu] : column[vu] + K].bitcast(FP8X4),
+                    rhs_scale=w_scales[:, column[vu] : column[vu] + K],
+                    start=(passes[v] == 0),
+                    stop=(passes[v] == SIDE - 1),
                 )
-            if uh == 1 and v >= 1:
+                passes[v] += 1
+            if passes[v] == SIDE and v >= 1:
                 combine(v - 1)
         combine(SIDE - 1)

@@ -125,11 +125,15 @@ def tile_iwht3layer_pa_s_kernel(tc, trans, weight, bias, out):
                     out=both[:, u - 1, :, 0, :].bitcast(F32).rearrange("c g (j h) -> c g j h", h=2),
                     in_=x_bank[:, : 2 * P].rearrange("c (h g j) -> c g j h", h=2, j=SIDE),
                 )
-        for u in range(SIDE):
-            quantise_x(u)
-            if u + 1 < SIDE:
-                negate(u + 1)
-                spread(u)
+        quantise_x(0)
+        negate(1)
+        negate(2)
+        quantise_x(1)
+        negate(3)
+        quantise_x(2)
+        spread(0)
+        quantise_x(3)
+        spread(1)
 
         bias_bank = psum.tile([P, BANK], F32, tag="half_3")
         nc.tensor.matmul(out=bias_bank[:, :K], lhsT=ones[:], rhs=bias_rows[:], start=True, stop=True)
@@ -197,7 +201,8 @@ def tile_iwht3layer_pa_s_kernel(tc, trans, weight, bias, out):
             if passes[v] == 0:
                 regroup(nc.vector.tensor_copy, v, SIDE - 1)
                 if v == 0:
-                    spread(SIDE - 1)
+                    spread(2)
+                    spread(3)
                     spread_scales()
             columns = slice(column[members[0]], column[members[0]] + len(members) * K)
             nc.vector.quantize_mx(

@@ -199,11 +199,14 @@ def tile_iwht3layer_pa_s_kernel(tc, trans, weight, bias, out):
         for n, members in enumerate(groups):
             v = members[0][0]
             if passes[v] == 0:
-                regroup(nc.vector.tensor_copy, v, SIDE - 1)
                 if v == 0:
+                    regroup(nc.vector.tensor_copy, 0, SIDE - 1)
                     spread(2)
+                    regroup(nc.vector.tensor_copy, 1, SIDE - 1)
                     spread(3)
                     spread_scales()
+                elif v + 1 < SIDE:
+                    regroup(nc.vector.tensor_copy, v + 1, SIDE - 1)
             columns = slice(column[members[0]], column[members[0]] + len(members) * K)
             nc.vector.quantize_mx(
                 out=w_codes[:, columns].bitcast(FP8X4),

@@ -155,15 +155,17 @@ def tile_iwht3layer_pa_s_kernel(tc, trans, weight, bias, out):
                 column[vu] = filled + slot * K
             filled += len(members) * K
 
-        def regroup(copy, v, u):
+        def regroup(copy, v, u, columns=slice(0, K)):
             copy(
-                out=grouped[v, u].rearrange("c (g i) s -> c g s i", i=4),
-                in_=w_raw[v, u // 2][:, u % 2, :].rearrange("c (s g i) -> c g s i", s=PACK, i=4),
+                out=grouped[v, u][:, columns, :].rearrange("c (g i) s -> c g s i", i=4),
+                in_=w_raw[v, u // 2][:, u % 2, :]
+                .rearrange("c (s k) -> c s k", s=PACK)[:, :, columns]
+                .rearrange("c s (g i) -> c g s i", i=4),
             )
 
         for v in range(SIDE):
             for u in range(SIDE - 1):
-                regroup(nc.scalar.copy, v, u)
+                regroup(nc.scalar.copy, v, u, slice(0, K // 2) if (v, u) == (SIDE - 1, SIDE - 2) else slice(0, K))
 
         w_codes = keep.tile([P, SIDE * SIDE * K], U32, align_bytes=64)
         w_scales = keep.tile([P, SIDE * SIDE * K], U8, align_bytes=64)
@@ -207,6 +209,8 @@ def tile_iwht3layer_pa_s_kernel(tc, trans, weight, bias, out):
                     spread_scales()
                 elif v + 1 < SIDE:
                     regroup(nc.vector.tensor_copy, v + 1, SIDE - 1)
+                    if v + 1 == SIDE - 1:
+                        regroup(nc.vector.tensor_copy, v + 1, SIDE - 2, slice(K // 2, K))
             columns = slice(column[members[0]], column[members[0]] + len(members) * K)
             nc.vector.quantize_mx(
                 out=w_codes[:, columns].bitcast(FP8X4),
@@ -225,6 +229,10 @@ def tile_iwht3layer_pa_s_kernel(tc, trans, weight, bias, out):
                     stop=(passes[v] == SIDE - 1),
                 )
                 passes[v] += 1
-            if passes[v] == SIDE and v >= 1:
+            if v in (1, 2) and passes[v] == SIDE:
                 combine(v - 1)
+            if v == SIDE - 1 and passes[v] == SIDE - 1:
+                combine(v - 1, (1,))
+            if v == SIDE - 1 and passes[v] == SIDE:
+                combine(v - 1, (-1,))
         combine(SIDE - 1)

@@ -31,7 +31,7 @@ def tile_iwht3layer_pa_s_kernel(tc, trans, weight, bias, out):
         psum = ctx.enter_context(tc.psum_pool(name="psum", bufs=1))
         ctx.enter_context(tc.manual_schedule())
 
-        pieces = [(v, uh) for v in range(SIDE) for uh in range(2)]
+        pieces = [(0, 1), (0, 0)] + [(v, uh) for v in range(1, SIDE) for uh in range(2)]
 
         x_rows = keep.tile([P, SIDE, C], BF16)
         x_view = trans.rearrange("(u v) b i j c -> (v b i j) u c", v=SIDE)
@@ -50,6 +50,30 @@ def tile_iwht3layer_pa_s_kernel(tc, trans, weight, bias, out):
         bias_rows = keep.tile([P, K], BF16)
         nc.vector.memset(bias_rows[:], 0.0)
         nc.scalar.dma_start(out=bias_rows[0:1, :], in_=bias.rearrange("a b c k -> (a b c) k"))
+
+        groups = []
+        groups.extend([[(0, 2), (0, 3)], [(0, 0), (0, 1)]])
+        for v in range(1, SIDE - 1):
+            groups.extend([[(v, 0), (v, 1)], [(v, 2), (v, 3)]])
+        groups.extend([[(SIDE - 1, 0), (SIDE - 1, 3)], [(SIDE - 1, 1)], [(SIDE - 1, 2)]])
+        group_tiles = []
+        grouped = {}
+        column = {}
+        filled = 0
+        for n, members in enumerate(groups):
+            group_tiles.append(keep.tile([P, len(members), K, PACK], BF16, name="grouped_%d" % n, align_bytes=64))
+            for slot, vu in enumerate(members):
+                grouped[vu] = group_tiles[n][:, slot]
+                column[vu] = filled + slot * K
+            filled += len(members) * K
+
+        def regroup(copy, v, u, columns=slice(0, K)):
+            copy(
+                out=grouped[v, u][:, columns, :].rearrange("c (g i) s -> c g s i", i=4),
+                in_=w_raw[v, u // 2][:, u % 2, :]
+                .rearrange("c (s k) -> c s k", s=PACK)[:, :, columns]
+                .rearrange("c s (g i) -> c g s i", i=4),
+            )
 
         x_words = x_rows[:].bitcast(F32).rearrange("m u (c4 h) -> m u h c4", h=2)
         GROUPS = SIDE * ROW_GROUPS
@@ -121,12 +145,14 @@ def tile_iwht3layer_pa_s_kernel(tc, trans, weight, bias, out):
                     in_=x_bank[:, : 2 * P].rearrange("c (h m) -> c m h", h=2),
                 )
             else:
-                nc.scalar.copy(
+                copy = nc.vector.tensor_copy if u == 1 else nc.scalar.copy
+                copy(
                     out=both[:, u - 1, :, 0, :].bitcast(F32).rearrange("c g (j h) -> c g j h", h=2),
                     in_=x_bank[:, : 2 * P].rearrange("c (h g j) -> c g j h", h=2, j=SIDE),
                 )
         quantise_x(0)
         negate(1)
+        regroup(nc.vector.tensor_copy, 0, SIDE - 1)
         negate(2)
         quantise_x(1)
         negate(3)
@@ -140,69 +166,43 @@ def tile_iwht3layer_pa_s_kernel(tc, trans, weight, bias, out):
         bias_all = keep.tile([P, K], F32)
         nc.scalar.copy(out=bias_all[:], in_=bias_bank[:, :K])
 
-        groups = []
-        for v in range(SIDE - 1):
-            groups.extend([[(v, 0), (v, 1)], [(v, 2), (v, 3)]])
-        groups.extend([[(SIDE - 1, 0), (SIDE - 1, 3)], [(SIDE - 1, 1)], [(SIDE - 1, 2)]])
-        group_tiles = []
-        grouped = {}
-        column = {}
-        filled = 0
-        for n, members in enumerate(groups):
-            group_tiles.append(keep.tile([P, len(members), K, PACK], BF16, name="grouped_%d" % n, align_bytes=64))
-            for slot, vu in enumerate(members):
-                grouped[vu] = group_tiles[n][:, slot]
-                column[vu] = filled + slot * K
-            filled += len(members) * K
-
-        def regroup(copy, v, u, columns=slice(0, K)):
-            copy(
-                out=grouped[v, u][:, columns, :].rearrange("c (g i) s -> c g s i", i=4),
-                in_=w_raw[v, u // 2][:, u % 2, :]
-                .rearrange("c (s k) -> c s k", s=PACK)[:, :, columns]
-                .rearrange("c s (g i) -> c g s i", i=4),
-            )
-
         for v in range(SIDE):
-            for u in range(SIDE - 1):
+            for u in (2, 0, 1) if v == 0 else (0, 1, 2):
                 regroup(nc.scalar.copy, v, u, slice(0, K // 2) if (v, u) == (SIDE - 1, SIDE - 2) else slice(0, K))
 
         w_codes = keep.tile([P, SIDE * SIDE * K], U32, align_bytes=64)
         w_scales = keep.tile([P, SIDE * SIDE * K], U8, align_bytes=64)
         half = [psum.tile([P, BANK], F32, name="half_%d" % v) for v in range(SIDE)]
-        total = [keep.tile([P, min(2**v, SIDE), K], F32, name="total_%d" % v) for v in range(SIDE)]
+        even = keep.tile([P, K], F32)
+        parts = keep.tile([P, 3, K], F32)
+        result = keep.tile([P, SIDE, K], F32)
 
         out_view = out.rearrange("b (i p) (j q) k -> (b i p j) q k", p=SIDE, q=SIDE)
 
-        def combine(v, signs=(1, -1)):
-            if v == 0:
-                nc.vector.scalar_tensor_tensor(
-                    out=total[0][:, 0, :], in0=half[0][:, :K], scalar=1.0 / 16.0, in1=bias_all[:], op0=ALU.mult, op1=ALU.add
-                )
-            if v == 1:
-                for q in range(2):
-                    nc.vector.scalar_tensor_tensor(
-                        out=total[1][:, q, :], in0=half[1][:, :K], scalar=HAD[q][1] / 16.0, in1=total[0][:, 0, :],
-                        op0=ALU.mult, op1=ALU.add,
-                    )
-            if v >= 2:
-                twice = half[v][:, :K].unsqueeze(1).to_broadcast([P, 2, K])
-                for sign in signs:
-                    first, second = [q for q in range(SIDE) if HAD[q][v] == sign]
-                    pair = slice(first, second + 1, second - first)
-                    before = total[1][:] if v == 2 else total[2][:, pair, :]
-                    nc.vector.scalar_tensor_tensor(
-                        out=total[v][:, pair, :], in0=twice, scalar=sign / 16.0, in1=before, op0=ALU.mult, op1=ALU.add
-                    )
-                    if v == SIDE - 1:
-                        nc.sync.dma_start(out=out_view[:, pair, :], in_=total[v][:, pair, :])
+        def add(out, source, factor, before):
+            nc.vector.scalar_tensor_tensor(out=out, in0=source, scalar=factor / 16.0, in1=before, op0=ALU.mult, op1=ALU.add)
 
+        def combine(step):
+            if step == 0:
+                add(parts[:, 1, :], half[0][:, :K], 1.0, bias_all[:])
+            if step == 1:
+                add(even[:], half[1][:, :K], -2.0, parts[:, 1, :])
+            if step == 2:
+                add(parts[:, 0, :], half[2][:, :K], 2.0, even[:])
+            if step == 3:
+                add(parts[:, 2, :], half[2][:, :K], -2.0, even[:])
+            if step == 4:
+                twice = half[3][:, :K].unsqueeze(1).to_broadcast([P, 2, K])
+                for sign, pair, before in ((-1.0, slice(1, 3), parts[:, :2, :]), (1.0, slice(0, 4, 3), parts[:, 1:, :])):
+                    add(result[:, pair, :], twice, sign, before)
+                    nc.sync.dma_start(out=out_view[:, pair, :], in_=result[:, pair, :])
+
+        AFTER = {5: 0, 6: 1, 8: 2}
         passes = [0] * SIDE
         for n, members in enumerate(groups):
             v = members[0][0]
-            if passes[v] == 0:
+            if members == groups[2 * v]:
                 if v == 0:
-                    regroup(nc.vector.tensor_copy, 0, SIDE - 1)
                     spread(2)
                     regroup(nc.vector.tensor_copy, 1, SIDE - 1)
                     spread(3)
@@ -219,20 +219,18 @@ def tile_iwht3layer_pa_s_kernel(tc, trans, weight, bias, out):
             )
             for vu in members:
                 u = vu[1]
-                nc.tensor.matmul_mx(
-                    out=half[v][:, :K],
-                    lhsT=x_codes[:, u, v * P : (v + 1) * P].bitcast(FP8X4),
-                    lhsT_scale=x_scales[:, u, v * P : (v + 1) * P],
-                    rhs=w_codes[:, column[vu] : column[vu] + K].bitcast(FP8X4),
-                    rhs_scale=w_scales[:, column[vu] : column[vu] + K],
-                    start=(passes[v] == 0),
-                    stop=(passes[v] == SIDE - 1),
-                )
-                passes[v] += 1
-            if v in (1, 2) and passes[v] == SIDE:
-                combine(v - 1)
-            if v == SIDE - 1 and passes[v] == SIDE - 1:
-                combine(v - 1, (1,))
-            if v == SIDE - 1 and passes[v] == SIDE:
-                combine(v - 1, (-1,))
-        combine(SIDE - 1)
+                for bank in [[0], [1, 0], [2, 3], [3]][v]:
+                    nc.tensor.matmul_mx(
+                        out=half[bank][:, :K],
+                        lhsT=x_codes[:, u, v * P : (v + 1) * P].bitcast(FP8X4),
+                        lhsT_scale=x_scales[:, u, v * P : (v + 1) * P],
+                        rhs=w_codes[:, column[vu] : column[vu] + K].bitcast(FP8X4),
+                        rhs_scale=w_scales[:, column[vu] : column[vu] + K],
+                        start=(passes[bank] == 0),
+                        stop=(passes[bank] == (3 if bank in (1, 2) else 7)),
+                    )
+                    passes[bank] += 1
+            if n in AFTER:
+                combine(AFTER[n])
+        combine(3)
+        combine(4)

from contextlib import ExitStack

import concourse.mybir as mybir
from concourse.masks import make_identity

F32 = mybir.dt.float32
BF16 = mybir.dt.bfloat16
U32 = mybir.dt.uint32
I32 = mybir.dt.int32
U8 = mybir.dt.uint8
FP8X4 = mybir.dt.float8_e4m3fn_x4
ALU = mybir.AluOpType

P = 128
PACK = 4
SIDE = 4
ROWS = 32
ROW_GROUPS = 8
C = 512
K = 128
BANK = 512
HAD = ((1, 1, 1, 1), (1, -1, 1, -1), (1, 1, -1, -1), (1, -1, -1, 1))

FLOPS = 2 * SIDE * SIDE * ROWS * C * K


def tile_iwht3layer_pa_s_kernel(tc, trans, weight, bias, out):
    nc = tc.nc
    with ExitStack() as ctx:
        keep = ctx.enter_context(tc.tile_pool(name="keep", bufs=1))
        psum = ctx.enter_context(tc.psum_pool(name="psum", bufs=1))
        ctx.enter_context(tc.manual_schedule())

        pieces = [(0, 1), (0, 0)] + [(v, uh) for v in range(1, SIDE) for uh in range(2)]

        x_rows = keep.tile([P, SIDE, C], BF16)
        x_view = trans.rearrange("(u v) b i j c -> (v b i j) u c", v=SIDE)
        for u in range(SIDE):
            nc.sync.dma_start(out=x_rows[:, u, :], in_=x_view[:, u, :])
        w_view = weight.rearrange("(u v) (c4 s) k -> v c4 u (s k)", v=SIDE, s=PACK)
        w_raw = {}
        for v, uh in pieces:
            w_raw[v, uh] = keep.tile([P, 2, PACK * K], BF16, name="w_raw_%d_%d" % (v, uh))
            nc.sync.dma_start(out=w_raw[v, uh][:], in_=w_view[v, :, 2 * uh : 2 * uh + 2, :])

        identity = keep.tile([P, P], F32)
        make_identity(nc, identity[:])
        ones = keep.tile([P, P], BF16)
        nc.vector.memset(ones[:], 1.0)
        bias_rows = keep.tile([P, K], BF16)
        nc.vector.memset(bias_rows[:], 0.0)
        nc.scalar.dma_start(out=bias_rows[0:1, :], in_=bias.rearrange("a b c k -> (a b c) k"))

        groups = []
        groups.extend([[(0, 2), (0, 3)], [(0, 0), (0, 1)]])
        for v in range(1, SIDE - 1):
            groups.extend([[(v, 0), (v, 1)], [(v, 2), (v, 3)]])
        groups.extend([[(SIDE - 1, 0), (SIDE - 1, 3)], [(SIDE - 1, 1)], [(SIDE - 1, 2)]])
        group_tiles = []
        grouped = {}
        column = {}
        filled = 0
        for n, members in enumerate(groups):
            group_tiles.append(keep.tile([P, len(members), K, PACK], BF16, name="grouped_%d" % n, align_bytes=64))
            for slot, vu in enumerate(members):
                grouped[vu] = group_tiles[n][:, slot]
                column[vu] = filled + slot * K
            filled += len(members) * K

        def regroup(copy, v, u, columns=slice(0, K)):
            copy(
                out=grouped[v, u][:, columns, :].rearrange("c (g i) s -> c g s i", i=4),
                in_=w_raw[v, u // 2][:, u % 2, :]
                .rearrange("c (s k) -> c s k", s=PACK)[:, :, columns]
                .rearrange("c s (g i) -> c g s i", i=4),
            )

        x_words = x_rows[:].bitcast(F32).rearrange("m u (c4 h) -> m u h c4", h=2)
        GROUPS = SIDE * ROW_GROUPS
        plain = keep.tile([P, P * PACK], BF16, align_bytes=64)
        plain_codes = keep.tile([P, P], I32, align_bytes=64)
        plain_scales = keep.tile([P, P], U8, align_bytes=64)
        both = keep.tile([P, SIDE - 1, GROUPS, 2, SIDE * PACK], BF16, align_bytes=64)
        both_codes = keep.tile([P, SIDE - 1, GROUPS, 2, SIDE], I32, align_bytes=64)
        both_scales = keep.tile([P, SIDE - 1, GROUPS * 2 * SIDE], U8, align_bytes=64)
        nc.vector.memset(plain_scales[:].bitcast(I32), 0)
        nc.vector.memset(both_scales[:].bitcast(I32), 0)
        x_codes = keep.tile([P, SIDE, SIDE * P], I32, align_bytes=64)
        x_scales = keep.tile([P, SIDE, SIDE * P], U8, align_bytes=64)

        def negate(u):
            nc.vector.tensor_scalar_mul(out=both[:, u - 1, :, 1, :], in0=both[:, u - 1, :, 0, :], scalar1=-1.0)

        def quantise_x(u):
            if u == 0:
                nc.vector.quantize_mx(out=plain_codes[:].bitcast(FP8X4), scales=plain_scales[:], in_=plain[:])
            else:
                nc.vector.quantize_mx(
                    out=both_codes[:, u - 1].rearrange("c g n j -> c (g n j)").bitcast(FP8X4),
                    scales=both_scales[:, u - 1, :],
                    in_=both[:, u - 1].rearrange("c g n e -> c (g n e)"),
                )

        def spread(u):
            codes = x_codes[:, u, :]
            if u == 0:
                nc.vector.tensor_copy(
                    out=codes.rearrange("c (g p j) -> c g p j", p=SIDE, j=SIDE),
                    in_=plain_codes[:].rearrange("c (g j) -> c g j", j=SIDE).unsqueeze(2).to_broadcast([P, GROUPS, SIDE, SIDE]),
                )
            if u == 1:
                nc.vector.tensor_copy(
                    out=codes.rearrange("c (g a e) -> c g a e", a=2, e=2 * SIDE),
                    in_=both_codes[:, 0].rearrange("c g n j -> c g (n j)").unsqueeze(2).to_broadcast([P, GROUPS, 2, 2 * SIDE]),
                )
            if u == 2:
                nc.vector.tensor_copy(
                    out=codes.rearrange("c (m a j) -> c m a j", a=2, j=SIDE),
                    in_=both_codes[:, 1].rearrange("c g n j -> c (g n) j").unsqueeze(2).to_broadcast([P, 2 * GROUPS, 2, SIDE]),
                )
            if u == 3:
                for n, where in enumerate((slice(0, SIDE, SIDE - 1), slice(1, SIDE - 1))):
                    nc.vector.tensor_copy(
                        out=codes.rearrange("c (g p j) -> c g p j", p=SIDE, j=SIDE)[:, :, where, :],
                        in_=both_codes[:, 2, :, n, :].unsqueeze(2).to_broadcast([P, GROUPS, 2, SIDE]),
                    )

        def spread_scales():
            nc.vector.tensor_copy(
                out=x_scales[:, 0, :].bitcast(I32).rearrange("c (g p) -> c g p", p=SIDE),
                in_=plain_scales[:].bitcast(I32).unsqueeze(2).to_broadcast([P, GROUPS, SIDE]),
            )
            nc.vector.tensor_copy(
                out=x_scales[:, 1:, :].bitcast(I32).rearrange("c u (g p) -> c u g p", p=SIDE),
                in_=both_scales[:].bitcast(I32).rearrange("c u (g n) -> c u g n", n=2)[:, :, :, 0:1].to_broadcast([P, SIDE - 1, GROUPS, SIDE]),
            )

        for u in range(SIDE):
            x_bank = psum.tile([P, BANK], F32, tag="x_bank_%d" % u)
            for h in range(2):
                nc.tensor.transpose(x_bank[:, h * P : (h + 1) * P], x_words[:, u, h, :], identity[:])
            if u == 0:
                nc.scalar.copy(
                    out=plain[:].bitcast(F32).rearrange("c (m h) -> c m h", h=2),
                    in_=x_bank[:, : 2 * P].rearrange("c (h m) -> c m h", h=2),
                )
            else:
                copy = nc.vector.tensor_copy if u == 1 else nc.scalar.copy
                copy(
                    out=both[:, u - 1, :, 0, :].bitcast(F32).rearrange("c g (j h) -> c g j h", h=2),
                    in_=x_bank[:, : 2 * P].rearrange("c (h g j) -> c g j h", h=2, j=SIDE),
                )
        quantise_x(0)
        negate(1)
        regroup(nc.vector.tensor_copy, 0, SIDE - 1)
        negate(2)
        quantise_x(1)
        negate(3)
        quantise_x(2)
        spread(0)
        quantise_x(3)
        spread(1)

        bias_bank = psum.tile([P, BANK], F32, tag="half_3")
        nc.tensor.matmul(out=bias_bank[:, :K], lhsT=ones[:], rhs=bias_rows[:], start=True, stop=True)
        bias_all = keep.tile([P, K], F32)
        nc.scalar.copy(out=bias_all[:], in_=bias_bank[:, :K])

        for v in range(SIDE):
            for u in (2, 0, 1) if v == 0 else (0, 1, 2):
                regroup(nc.scalar.copy, v, u, slice(0, K // 2) if (v, u) == (SIDE - 1, SIDE - 2) else slice(0, K))

        w_codes = keep.tile([P, SIDE * SIDE * K], U32, align_bytes=64)
        w_scales = keep.tile([P, SIDE * SIDE * K], U8, align_bytes=64)
        half = [psum.tile([P, BANK], F32, name="half_%d" % v) for v in range(SIDE)]
        even = keep.tile([P, K], F32)
        parts = keep.tile([P, 3, K], F32)
        result = keep.tile([P, SIDE, K], F32)

        out_view = out.rearrange("b (i p) (j q) k -> (b i p j) q k", p=SIDE, q=SIDE)

        def add(out, source, factor, before):
            nc.vector.scalar_tensor_tensor(out=out, in0=source, scalar=factor / 16.0, in1=before, op0=ALU.mult, op1=ALU.add)

        def combine(step):
            if step == 0:
                add(parts[:, 1, :], half[0][:, :K], 1.0, bias_all[:])
            if step == 1:
                add(even[:], half[1][:, :K], -2.0, parts[:, 1, :])
            if step == 2:
                add(parts[:, 0, :], half[2][:, :K], 2.0, even[:])
            if step == 3:
                add(parts[:, 2, :], half[2][:, :K], -2.0, even[:])
            if step == 4:
                twice = half[3][:, :K].unsqueeze(1).to_broadcast([P, 2, K])
                for sign, pair, before in ((-1.0, slice(1, 3), parts[:, :2, :]), (1.0, slice(0, 4, 3), parts[:, 1:, :])):
                    add(result[:, pair, :], twice, sign, before)
                    nc.sync.dma_start(out=out_view[:, pair, :], in_=result[:, pair, :])

        AFTER = {5: 0, 6: 1, 8: 2}
        passes = [0] * SIDE
        for n, members in enumerate(groups):
            v = members[0][0]
            if members == groups[2 * v]:
                if v == 0:
                    spread(2)
                    regroup(nc.vector.tensor_copy, 1, SIDE - 1)
                    spread(3)
                    spread_scales()
                elif v + 1 < SIDE:
                    regroup(nc.vector.tensor_copy, v + 1, SIDE - 1)
                    if v + 1 == SIDE - 1:
                        regroup(nc.vector.tensor_copy, v + 1, SIDE - 2, slice(K // 2, K))
            columns = slice(column[members[0]], column[members[0]] + len(members) * K)
            nc.vector.quantize_mx(
                out=w_codes[:, columns].bitcast(FP8X4),
                scales=w_scales[:, columns],
                in_=group_tiles[n][:].rearrange("c u k s -> c (u k s)"),
            )
            for vu in members:
                u = vu[1]
                for bank in [[0], [1, 0], [2, 3], [3]][v]:
                    nc.tensor.matmul_mx(
                        out=half[bank][:, :K],
                        lhsT=x_codes[:, u, v * P : (v + 1) * P].bitcast(FP8X4),
                        lhsT_scale=x_scales[:, u, v * P : (v + 1) * P],
                        rhs=w_codes[:, column[vu] : column[vu] + K].bitcast(FP8X4),
                        rhs_scale=w_scales[:, column[vu] : column[vu] + K],
                        start=(passes[bank] == 0),
                        stop=(passes[bank] == (3 if bank in (1, 2) else 7)),
                    )
                    passes[bank] += 1
            if n in AFTER:
                combine(AFTER[n])
        combine(3)
        combine(4)
